import numpy as np
import ml_dtypes


def mxq(x, axis, fmt="e4m3"):
    dtype, down = {"e4m3": (ml_dtypes.float8_e4m3fn, 7), "e5m2": (ml_dtypes.float8_e5m2, 14)}[fmt]
    v = np.moveaxis(np.asarray(x, np.float32).astype(ml_dtypes.bfloat16).astype(np.float64), axis, -1)
    blocks = v.reshape(v.shape[:-1] + (-1, 32))
    amax = np.abs(blocks).max(-1, keepdims=True)
    byte = np.maximum(np.where(amax > 0, np.frexp(amax)[1] - 1 + 127, 0) - down, 1)
    scale = np.exp2(byte - 127.0)
    codes = (blocks / scale).astype(np.float32).astype(dtype).astype(np.float64)
    return np.moveaxis((codes * scale).reshape(v.shape), -1, axis)


WIDE = False


def mx_kscale(k):
    if not WIDE:
        return np.ones(k)
    levels = np.array([10, -10, 5, -5, 0])
    a = np.random.permutation(np.resize(levels, k // 512 * 4)).reshape(k // 512, 4)
    idx = np.arange(k)
    return np.exp2(a[idx // 512, idx % 128 // 32])


BF16 = ml_dtypes.bfloat16


def bf(x):
    return np.asarray(x, np.float32).astype(BF16)


def f64(x):
    return np.asarray(x).astype(np.float64)


B, S, DIM, H, NOPE, ROPE_D, VD = 4, 1024, 1024, 2, 64, 64, 128
QKD = NOPE + ROPE_D
BASE = 10000.0


def rope_cos_sin(seq_len):
    theta = 1.0 / BASE ** (f64(np.arange(0, ROPE_D, 2)) / ROPE_D)
    pos = f64(np.arange(seq_len))
    ang = pos[:, None] * theta[None, :]
    return np.cos(ang), np.sin(ang)


def apply_rope(v, cos, sin):
    b, s, h, d = v.shape
    vs = v.reshape(b, s, h, d // 2, 2)
    c = cos[None, :, None, :]
    sn = sin[None, :, None, :]
    out = np.stack([vs[..., 0] * c - vs[..., 1] * sn, vs[..., 1] * c + vs[..., 0] * sn], axis=-1)
    return out.reshape(b, s, h, d)


def setup_inputs():
    s = mx_kscale(DIM)
    return {'x': bf(np.random.standard_normal((B, S, DIM)) * s),
            'Wq': bf(np.random.standard_normal((DIM, H * QKD)) / np.sqrt(DIM) / s[:, None]),
            'Wk': bf(np.random.standard_normal((DIM, H * QKD)) / np.sqrt(DIM) / s[:, None])}


def reference(x, Wq, Wk):
    xq = mxq(f64(x), 2, 'e4m3')
    q = (xq @ mxq(f64(Wq), 0, 'e4m3')).reshape(B, S, H, QKD)
    k = (xq @ mxq(f64(Wk), 0, 'e4m3')).reshape(B, S, H, QKD)
    cos, sin = rope_cos_sin(S)
    q = np.concatenate([q[..., :NOPE], apply_rope(q[..., NOPE:], cos, sin)], axis=-1)
    k = np.concatenate([k[..., :NOPE], apply_rope(k[..., NOPE:], cos, sin)], axis=-1)
    return q, k

@@ -1,0 +1,202 @@
+import math
+from contextlib import ExitStack
+
+import concourse.mybir as mybir
+from concourse.masks import make_identity
+
+F32 = mybir.dt.float32
+BF16 = mybir.dt.bfloat16
+I32 = mybir.dt.int32
+U32 = mybir.dt.uint32
+U8 = mybir.dt.uint8
+FP8X4 = mybir.dt.float8_e4m3fn_x4
+ALU = mybir.AluOpType
+ACT = mybir.ActivationFunctionType
+
+P = 128
+B = 4
+T = 8
+DIM = 1024
+NPAIRS = 32
+RATIO = 10000.0 ** (-1.0 / 32.0)
+ROPE = 0
+NOPE = 1
+FLOPS = 2 * 4096 * 1024 * 512
+
+MANUAL = True
+GP_ADD_UNTIL = 15
+
+
+def tile_mla_pa_t_kernel(tc, x, Wq, Wk, out_0, out_1):
+    nc = tc.nc
+    with ExitStack() as ctx:
+        if MANUAL:
+            ctx.enter_context(tc.manual_schedule())
+        keep = ctx.enter_context(tc.tile_pool(name="keep", bufs=1))
+        work = ctx.enter_context(tc.tile_pool(name="work", bufs=3))
+        ps_t = ctx.enter_context(tc.psum_pool(name="ps_t", bufs=4))
+        ps_r = ctx.enter_context(tc.psum_pool(name="ps_r", bufs=2))
+        ps_n = ctx.enter_context(tc.psum_pool(name="ps_n", bufs=2))
+
+        x_view = x.rearrange("b (p t) k -> b p t k", t=T)
+        out_views = [o.rearrange("b (p t) h d -> b p t (h d)", t=T) for o in (out_0, out_1)]
+
+        chunks = [(0, 0, 2), (0, 2, 2), (0, 4, 4), (1, 0, 8), (2, 0, 8), (3, 0, 8)]
+        x_words = {}
+        wraw = keep.tile([P, 2, 8, 256], BF16, name="wraw")
+
+        def load_x(b, t0, nt):
+            xs = keep.tile([P, nt, DIM], BF16, name="x%d_%d" % (b, t0))
+            nc.sync.dma_start(out=xs[:], in_=x_view[b][:, t0 : t0 + nt, :])
+            for t in range(nt):
+                x_words[(b, t0 + t)] = xs[:, t, :].bitcast(F32)
+
+        load_x(*chunks[0])
+        for g in range(2):
+            for qk, w_dram in enumerate((Wq, Wk)):
+                nc.sync.dma_start(
+                    out=wraw[:, qk, 4 * g : 4 * g + 4, :].rearrange("p (u e) c -> p u e c", e=2),
+                    in_=w_dram.rearrange("(j q e) c -> q j e c", j=4, e=2)[:, 2 * g : 2 * g + 2],
+                )
+        for chunk in chunks[1:]:
+            load_x(*chunk)
+
+        zero = keep.tile([P, 1], F32, name="zero")
+        nc.vector.memset(zero[:], 0.0)
+        warm = keep.tile([P, 1], F32, name="warm")
+        nc.scalar.activation(out=warm[:], in_=zero[:], func=ACT.Sin)
+        pos_i = keep.tile([P, T], I32, name="pos_i")
+        nc.gpsimd.iota(pos_i[:], pattern=[[1, T]], base=0, channel_multiplier=T)
+        ident = keep.tile([P, P], F32, name="ident")
+        make_identity(nc, ident[:])
+
+        turns = keep.tile([P, T, NPAIRS], F32, name="turns")
+        nc.vector.tensor_scalar(
+            out=turns[:, :, 0:1], in0=pos_i[:].unsqueeze(2), scalar1=1.0 / (2.0 * math.pi), scalar2=None, op0=ALU.mult
+        )
+        for level in range(5):
+            w = 1 << level
+            nc.vector.tensor_scalar(
+                out=turns[:, :, w : 2 * w], in0=turns[:, :, 0:w], scalar1=RATIO**w, scalar2=None, op0=ALU.mult
+            )
+        whole = keep.tile([P, 2, T, NPAIRS], I32, name="whole")
+        nc.vector.tensor_scalar(out=whole[:, 0], in0=turns[:], scalar1=0.25, scalar2=None, op0=ALU.add)
+        nc.vector.tensor_copy(out=whole[:, 1], in_=turns[:])
+        frac = keep.tile([P, 2, T, NPAIRS], F32, name="frac")
+        nc.vector.tensor_tensor(out=frac[:, 0], in0=whole[:, 0], in1=turns[:], op=ALU.subtract)
+        nc.vector.scalar_tensor_tensor(
+            out=frac[:, 1], in0=whole[:, 1], scalar=0.25, in1=turns[:], op0=ALU.add, op1=ALU.subtract
+        )
+        half_sin = keep.tile([P, 2, T, NPAIRS], F32, name="half_sin")
+        nc.scalar.activation(out=half_sin[:], in_=frac[:], func=ACT.Sin, scale=math.pi)
+        half_sq = keep.tile([P, 2, T, NPAIRS], F32, name="half_sq")
+        nc.scalar.activation(out=half_sq[:], in_=half_sin[:], func=ACT.Square)
+        cos2 = keep.tile([P, T, 2 * NPAIRS], F32, name="cos2")
+        nc.vector.tensor_scalar(
+            out=cos2[:].rearrange("p t (i e) -> p t i e", e=2),
+            in0=half_sq[:, 0].unsqueeze(3).to_broadcast([P, T, NPAIRS, 2]),
+            scalar1=-2.0,
+            scalar2=1.0,
+            op0=ALU.mult,
+            op1=ALU.add,
+        )
+        sin_pm = keep.tile([P, 2, T, NPAIRS], F32, name="sin_pm")
+        nc.vector.tensor_scalar(
+            out=sin_pm[:, 0], in0=half_sq[:, 1], scalar1=2.0, scalar2=-1.0, op0=ALU.mult, op1=ALU.add
+        )
+        nc.vector.tensor_scalar(
+            out=sin_pm[:, 1], in0=half_sq[:, 1], scalar1=-2.0, scalar2=1.0, op0=ALU.mult, op1=ALU.add
+        )
+
+        wgrp = keep.tile([P, 2, 2, 2, 2, 64, 4], BF16, name="wgrp", align_bytes=64)
+        wcodes = keep.tile([P, 2, 512], U32, name="wcodes", align_bytes=64)
+        wscales = keep.tile([P, 2, 512], U8, name="wscales", align_bytes=64)
+        for g in range(2):
+            for s in (ROPE, NOPE):
+                for qk in range(2):
+                    src = wraw[:, qk, 4 * g : 4 * g + 4, :].rearrange("p t (h s c) -> p t h s c", h=2, s=2)
+                    nc.vector.tensor_copy(
+                        out=wgrp[:, g, s, qk], in_=src[:, :, :, 1 - s, :].rearrange("p t h c -> p h c t")
+                    )
+            nc.vector.quantize_mx(
+                out=wcodes[:, g, :].bitcast(FP8X4),
+                scales=wscales[:, g, :],
+                in_=wgrp[:, g].rearrange("p s q h c t -> p (s q h c t)"),
+            )
+
+        out_sb = [keep.tile([P, 2, T, 256], F32, name="out_sb%d" % b) for b in range(B)]
+        stores = {1: (0, 0, 4), 3: (0, 4, 4), 5: (1, 0, 4), 7: (1, 4, 4), 9: (2, 0, 4), 11: (2, 4, 4),
+                  13: (3, 0, 4), 14: (3, 4, 2), 15: (3, 6, 2)}
+        quantised = {}
+
+        def prepare(n):
+            b, t0 = n // 4, 2 * (n % 4)
+            grp = work.tile([P, 2, 2, P, 4], BF16, name="grp", align_bytes=64)
+            grp_words = grp[:].bitcast(F32)
+            for a in range(2):
+                xt = ps_t.tile([P, 4, P], F32, name="xt")
+                for j in range(4):
+                    nc.tensor.transpose(
+                        out=xt[:, j, :], in_=x_words[(b, t0 + a)][:, P * j : P * (j + 1)], identity=ident[:]
+                    )
+                nc.scalar.copy(out=grp_words[:, a], in_=xt[:].rearrange("p (g u) r -> p g r u", u=2))
+            codes = work.tile([P, 512], U32, name="codes", align_bytes=64)
+            scales = work.tile([P, 512], U8, name="scales", align_bytes=64)
+            nc.vector.quantize_mx(
+                out=codes[:].bitcast(FP8X4), scales=scales[:], in_=grp[:].rearrange("p a g r t -> p (a g r t)")
+            )
+            quantised[n] = (codes, scales)
+
+        def finish(n):
+            b, t0 = n // 4, 2 * (n % 4)
+            codes, scales = quantised[n]
+            rope = ps_r.tile([P, 512], F32, name="rope")
+            nope = ps_n.tile([P, 512], F32, name="nope")
+            for a in range(2):
+                for s, bank in ((ROPE, rope), (NOPE, nope)):
+                    for g in range(2):
+                        col = (2 * a + g) * P
+                        nc.tensor.matmul_mx(
+                            out=bank[:, 256 * a : 256 * a + 256],
+                            lhsT=codes[:, col : col + P].bitcast(FP8X4),
+                            lhsT_scale=scales[:, col : col + P],
+                            rhs=wcodes[:, g, 256 * s : 256 * s + 256].bitcast(FP8X4),
+                            rhs_scale=wscales[:, g, 256 * s : 256 * s + 256],
+                            start=(g == 0),
+                            stop=(g == 1),
+                        )
+            cross = work.tile([P, 2, 2, 2, 2, NPAIRS], F32, name="cross")
+            nope_v = nope[:].rearrange("p (a q h c) -> p a q h c", a=2, q=2, h=2)
+            rope_v = rope[:].rearrange("p (a q h c) -> p a q h c", a=2, q=2, h=2)
+            rope_e = rope[:].rearrange("p (a q h i e) -> p a q h i e", a=2, q=2, h=2, e=2)
+            cos_b = cos2[:, t0 : t0 + 2, :].unsqueeze(2).to_broadcast([P, 2, 2, 2 * NPAIRS])
+            for qk in range(2):
+                dst = out_sb[b][:, qk, t0 : t0 + 2, :].rearrange("p a (h s c) -> p a h s c", h=2, s=2)
+                nc.scalar.copy(out=dst[:, :, :, 0, :], in_=nope_v[:, :, qk])
+                nc.vector.tensor_tensor(out=dst[:, :, :, 1, :], in0=rope_v[:, :, qk], in1=cos_b, op=ALU.mult)
+                for e in range(2):
+                    sin_b = sin_pm[:, e, t0 : t0 + 2, :].unsqueeze(2).to_broadcast([P, 2, 2, NPAIRS])
+                    nc.vector.tensor_tensor(
+                        out=cross[:, e, qk], in0=rope_e[:, :, qk, :, :, 1 - e], in1=sin_b, op=ALU.mult
+                    )
+            for qk in range(2):
+                rot = out_sb[b][:, qk, t0 : t0 + 2, :].rearrange("p a (h s i e) -> p (a h) s i e", h=2, s=2, e=2)
+                eng = nc.gpsimd if n < GP_ADD_UNTIL else nc.vector
+                eng.tensor_tensor(
+                    out=rot[:, :, 1],
+                    in0=rot[:, :, 1],
+                    in1=cross[:, :, qk].rearrange("p e a h i -> p (a h) i e"),
+                    op=ALU.add,
+                )
+            if n in stores:
+                sb, st0, snt = stores[n]
+                for qk in range(2):
+                    nc.sync.dma_start(
+                        out=out_views[qk][sb][:, st0 : st0 + snt, :], in_=out_sb[sb][:, qk, st0 : st0 + snt, :]
+                    )
+
+        prepare(0)
+        for n in range(16):
+            if n + 1 < 16:
+                prepare(n + 1)
+            finish(n)

@@ -23,17 +23,17 @@ ROPE = 0
 NOPE = 1
 FLOPS = 2 * 4096 * 1024 * 512
 
-MANUAL = True
+N_UNITS = 16
 GP_ADD_UNTIL = 15
+S_REGROUP = ((1, 1, 0), (1, 1, 1))
 
 
 def tile_mla_pa_t_kernel(tc, x, Wq, Wk, out_0, out_1):
     nc = tc.nc
     with ExitStack() as ctx:
-        if MANUAL:
-            ctx.enter_context(tc.manual_schedule())
+        ctx.enter_context(tc.manual_schedule())
         keep = ctx.enter_context(tc.tile_pool(name="keep", bufs=1))
-        work = ctx.enter_context(tc.tile_pool(name="work", bufs=3))
+        work = ctx.enter_context(tc.tile_pool(name="work", bufs=4))
         ps_t = ctx.enter_context(tc.psum_pool(name="ps_t", bufs=4))
         ps_r = ctx.enter_context(tc.psum_pool(name="ps_r", bufs=2))
         ps_n = ctx.enter_context(tc.psum_pool(name="ps_n", bufs=2))
@@ -41,25 +41,20 @@ def tile_mla_pa_t_kernel(tc, x, Wq, Wk, out_0, out_1):
         x_view = x.rearrange("b (p t) k -> b p t k", t=T)
         out_views = [o.rearrange("b (p t) h d -> b p t (h d)", t=T) for o in (out_0, out_1)]
 
-        chunks = [(0, 0, 2), (0, 2, 2), (0, 4, 4), (1, 0, 8), (2, 0, 8), (3, 0, 8)]
+        chunks = [(0, 0, 1), (0, 1, 1), (0, 2, 2), (0, 4, 2), (0, 6, 2), (1, 0, 4), (1, 4, 4), (2, 0, 8), (3, 0, 8)]
         x_words = {}
         wraw = keep.tile([P, 2, 8, 256], BF16, name="wraw")
-
-        def load_x(b, t0, nt):
-            xs = keep.tile([P, nt, DIM], BF16, name="x%d_%d" % (b, t0))
-            nc.sync.dma_start(out=xs[:], in_=x_view[b][:, t0 : t0 + nt, :])
-            for t in range(nt):
-                x_words[(b, t0 + t)] = xs[:, t, :].bitcast(F32)
-
-        load_x(*chunks[0])
         for g in range(2):
             for qk, w_dram in enumerate((Wq, Wk)):
                 nc.sync.dma_start(
                     out=wraw[:, qk, 4 * g : 4 * g + 4, :].rearrange("p (u e) c -> p u e c", e=2),
                     in_=w_dram.rearrange("(j q e) c -> q j e c", j=4, e=2)[:, 2 * g : 2 * g + 2],
                 )
-        for chunk in chunks[1:]:
-            load_x(*chunk)
+        for b, t0, nt in chunks:
+            xs = keep.tile([P, nt, DIM], BF16, name="x%d_%d" % (b, t0))
+            nc.sync.dma_start(out=xs[:], in_=x_view[b][:, t0 : t0 + nt, :])
+            for t in range(nt):
+                x_words[(b, t0 + t)] = xs[:, t, :].bitcast(F32)
 
         zero = keep.tile([P, 1], F32, name="zero")
         nc.vector.memset(zero[:], 0.0)
@@ -91,22 +86,28 @@ def tile_mla_pa_t_kernel(tc, x, Wq, Wk, out_0, out_1):
         nc.scalar.activation(out=half_sin[:], in_=frac[:], func=ACT.Sin, scale=math.pi)
         half_sq = keep.tile([P, 2, T, NPAIRS], F32, name="half_sq")
         nc.scalar.activation(out=half_sq[:], in_=half_sin[:], func=ACT.Square)
-        cos2 = keep.tile([P, T, 2 * NPAIRS], F32, name="cos2")
-        nc.vector.tensor_scalar(
-            out=cos2[:].rearrange("p t (i e) -> p t i e", e=2),
-            in0=half_sq[:, 0].unsqueeze(3).to_broadcast([P, T, NPAIRS, 2]),
-            scalar1=-2.0,
-            scalar2=1.0,
-            op0=ALU.mult,
-            op1=ALU.add,
-        )
-        sin_pm = keep.tile([P, 2, T, NPAIRS], F32, name="sin_pm")
-        nc.vector.tensor_scalar(
-            out=sin_pm[:, 0], in0=half_sq[:, 1], scalar1=2.0, scalar2=-1.0, op0=ALU.mult, op1=ALU.add
-        )
-        nc.vector.tensor_scalar(
-            out=sin_pm[:, 1], in0=half_sq[:, 1], scalar1=-2.0, scalar2=1.0, op0=ALU.mult, op1=ALU.add
-        )
+        cos_t = keep.tile([P, T, 2, 2 * NPAIRS], F32, name="cos_t")
+        sin_t = keep.tile([P, 2, T, 2, NPAIRS], F32, name="sin_t")
+
+        def tables():
+            for h in range(2):
+                nc.vector.tensor_scalar(
+                    out=cos_t[:, :, h, :].rearrange("p t (i e) -> p t i e", e=2),
+                    in0=half_sq[:, 0].unsqueeze(3).to_broadcast([P, T, NPAIRS, 2]),
+                    scalar1=-2.0,
+                    scalar2=1.0,
+                    op0=ALU.mult,
+                    op1=ALU.add,
+                )
+            for e, sign in ((0, -1.0), (1, 1.0)):
+                nc.vector.tensor_scalar(
+                    out=sin_t[:, e],
+                    in0=half_sq[:, 1].unsqueeze(2).to_broadcast([P, T, 2, NPAIRS]),
+                    scalar1=-2.0 * sign,
+                    scalar2=sign,
+                    op0=ALU.mult,
+                    op1=ALU.add,
+                )
 
         wgrp = keep.tile([P, 2, 2, 2, 2, 64, 4], BF16, name="wgrp", align_bytes=64)
         wcodes = keep.tile([P, 2, 512], U32, name="wcodes", align_bytes=64)
@@ -115,9 +116,11 @@ def tile_mla_pa_t_kernel(tc, x, Wq, Wk, out_0, out_1):
             for s in (ROPE, NOPE):
                 for qk in range(2):
                     src = wraw[:, qk, 4 * g : 4 * g + 4, :].rearrange("p t (h s c) -> p t h s c", h=2, s=2)
-                    nc.vector.tensor_copy(
-                        out=wgrp[:, g, s, qk], in_=src[:, :, :, 1 - s, :].rearrange("p t h c -> p h c t")
-                    )
+                    permuted = src[:, :, :, 1 - s, :].rearrange("p t h c -> p h c t")
+                    if (g, s, qk) in S_REGROUP:
+                        nc.scalar.copy(out=wgrp[:, g, s, qk], in_=permuted)
+                    else:
+                        nc.vector.tensor_copy(out=wgrp[:, g, s, qk], in_=permuted)
             nc.vector.quantize_mx(
                 out=wcodes[:, g, :].bitcast(FP8X4),
                 scales=wscales[:, g, :],
@@ -127,33 +130,50 @@ def tile_mla_pa_t_kernel(tc, x, Wq, Wk, out_0, out_1):
         out_sb = [keep.tile([P, 2, T, 256], F32, name="out_sb%d" % b) for b in range(B)]
         stores = {1: (0, 0, 4), 3: (0, 4, 4), 5: (1, 0, 4), 7: (1, 4, 4), 9: (2, 0, 4), 11: (2, 4, 4),
                   13: (3, 0, 4), 14: (3, 4, 2), 15: (3, 6, 2)}
-        quantised = {}
+        live = {}
 
-        def prepare(n):
-            b, t0 = n // 4, 2 * (n % 4)
-            grp = work.tile([P, 2, 2, P, 4], BF16, name="grp", align_bytes=64)
-            grp_words = grp[:].bitcast(F32)
+        def where(n):
+            return n // 4, 2 * (n % 4)
+
+        def transposes(n):
+            b, t0 = where(n)
             for a in range(2):
                 xt = ps_t.tile([P, 4, P], F32, name="xt")
                 for j in range(4):
                     nc.tensor.transpose(
                         out=xt[:, j, :], in_=x_words[(b, t0 + a)][:, P * j : P * (j + 1)], identity=ident[:]
                     )
-                nc.scalar.copy(out=grp_words[:, a], in_=xt[:].rearrange("p (g u) r -> p g r u", u=2))
+                live[("xt", n, a)] = xt
+
+        def regroup(n):
+            grp = work.tile([P, 2, 2, P, 4], BF16, name="grp", align_bytes=64)
+            grp_words = grp[:].bitcast(F32)
+            for a in range(2):
+                nc.scalar.copy(
+                    out=grp_words[:, a], in_=live[("xt", n, a)][:].rearrange("p (g u) r -> p g r u", u=2)
+                )
+            live[("grp", n)] = grp
+
+        def quantise(n, pieces):
+            grp = live[("grp", n)][:].rearrange("p a g r t -> p (a g r t)")
             codes = work.tile([P, 512], U32, name="codes", align_bytes=64)
             scales = work.tile([P, 512], U8, name="scales", align_bytes=64)
-            nc.vector.quantize_mx(
-                out=codes[:].bitcast(FP8X4), scales=scales[:], in_=grp[:].rearrange("p a g r t -> p (a g r t)")
-            )
-            quantised[n] = (codes, scales)
+            width = 512 // pieces
+            for piece in range(pieces):
+                cols = slice(piece * width, (piece + 1) * width)
+                nc.vector.quantize_mx(
+                    out=codes[:, cols].bitcast(FP8X4),
+                    scales=scales[:, cols],
+                    in_=grp[:, 4 * piece * width : 4 * (piece + 1) * width],
+                )
+            live[("q", n)] = (codes, scales)
 
-        def finish(n):
-            b, t0 = n // 4, 2 * (n % 4)
-            codes, scales = quantised[n]
+        def multiply(n):
+            codes, scales = live[("q", n)]
             rope = ps_r.tile([P, 512], F32, name="rope")
             nope = ps_n.tile([P, 512], F32, name="nope")
-            for a in range(2):
-                for s, bank in ((ROPE, rope), (NOPE, nope)):
+            for s, bank in ((ROPE, rope), (NOPE, nope)):
+                for a in range(2):
                     for g in range(2):
                         col = (2 * a + g) * P
                         nc.tensor.matmul_mx(
@@ -165,29 +185,48 @@ def tile_mla_pa_t_kernel(tc, x, Wq, Wk, out_0, out_1):
                             start=(g == 0),
                             stop=(g == 1),
                         )
+            live[("rope", n)] = rope
+            live[("nope", n)] = nope
+
+        def plain_out(n):
+            b, t0 = where(n)
+            dst = out_sb[b][:, :, t0 : t0 + 2, :].rearrange("p q a (h s c) -> p q a h s c", h=2, s=2)
+            nc.scalar.copy(
+                out=dst[:, :, :, :, 0, :],
+                in_=live[("nope", n)][:].rearrange("p (a q h c) -> p q a h c", a=2, q=2, h=2),
+            )
+
+        def products(n):
+            b, t0 = where(n)
+            rope = live[("rope", n)]
+            dst = out_sb[b][:, :, t0 : t0 + 2, :].rearrange("p q a (h s c) -> p q a h s c", h=2, s=2)
+            nc.vector.tensor_tensor(
+                out=dst[:, :, :, :, 1, :],
+                in0=rope[:].rearrange("p (a q h c) -> p q a h c", a=2, q=2, h=2),
+                in1=cos_t[:, t0 : t0 + 2].unsqueeze(1).to_broadcast([P, 2, 2, 2, 2 * NPAIRS]),
+                op=ALU.mult,
+            )
             cross = work.tile([P, 2, 2, 2, 2, NPAIRS], F32, name="cross")
-            nope_v = nope[:].rearrange("p (a q h c) -> p a q h c", a=2, q=2, h=2)
-            rope_v = rope[:].rearrange("p (a q h c) -> p a q h c", a=2, q=2, h=2)
-            rope_e = rope[:].rearrange("p (a q h i e) -> p a q h i e", a=2, q=2, h=2, e=2)
-            cos_b = cos2[:, t0 : t0 + 2, :].unsqueeze(2).to_broadcast([P, 2, 2, 2 * NPAIRS])
-            for qk in range(2):
-                dst = out_sb[b][:, qk, t0 : t0 + 2, :].rearrange("p a (h s c) -> p a h s c", h=2, s=2)
-                nc.scalar.copy(out=dst[:, :, :, 0, :], in_=nope_v[:, :, qk])
-                nc.vector.tensor_tensor(out=dst[:, :, :, 1, :], in0=rope_v[:, :, qk], in1=cos_b, op=ALU.mult)
-                for e in range(2):
-                    sin_b = sin_pm[:, e, t0 : t0 + 2, :].unsqueeze(2).to_broadcast([P, 2, 2, NPAIRS])
-                    nc.vector.tensor_tensor(
-                        out=cross[:, e, qk], in0=rope_e[:, :, qk, :, :, 1 - e], in1=sin_b, op=ALU.mult
-                    )
-            for qk in range(2):
-                rot = out_sb[b][:, qk, t0 : t0 + 2, :].rearrange("p a (h s i e) -> p (a h) s i e", h=2, s=2, e=2)
-                eng = nc.gpsimd if n < GP_ADD_UNTIL else nc.vector
-                eng.tensor_tensor(
-                    out=rot[:, :, 1],
-                    in0=rot[:, :, 1],
-                    in1=cross[:, :, qk].rearrange("p e a h i -> p (a h) i e"),
-                    op=ALU.add,
+            rope_e = rope[:].rearrange("p (a q h i e) -> p q a h i e", a=2, q=2, h=2, e=2)
+            for e in range(2):
+                nc.vector.tensor_tensor(
+                    out=cross[:, e],
+                    in0=rope_e[:, :, :, :, :, 1 - e],
+                    in1=sin_t[:, e, t0 : t0 + 2].unsqueeze(1).to_broadcast([P, 2, 2, 2, NPAIRS]),
+                    op=ALU.mult,
                 )
+            live[("cross", n)] = cross
+
+        def add_and_store(n):
+            b, t0 = where(n)
+            rot = out_sb[b][:, :, t0 : t0 + 2, :].rearrange("p q a (h s i e) -> p q (a h) s i e", h=2, s=2, e=2)
+            eng = nc.gpsimd if n < GP_ADD_UNTIL else nc.vector
+            eng.tensor_tensor(
+                out=rot[:, :, :, 1],
+                in0=rot[:, :, :, 1],
+                in1=live[("cross", n)][:].rearrange("p e q a h i -> p q (a h) i e"),
+                op=ALU.add,
+            )
             if n in stores:
                 sb, st0, snt = stores[n]
                 for qk in range(2):
@@ -195,8 +234,27 @@ def tile_mla_pa_t_kernel(tc, x, Wq, Wk, out_0, out_1):
                         out=out_views[qk][sb][:, st0 : st0 + snt, :], in_=out_sb[sb][:, qk, st0 : st0 + snt, :]
                     )
 
-        prepare(0)
-        for n in range(16):
-            if n + 1 < 16:
-                prepare(n + 1)
-            finish(n)
+        blocks = [((0, 1), (0,)), ((2, 3), (1,))]
+        blocks += [((n + 2, n + 3), (n, n + 1)) for n in range(2, N_UNITS - 2, 2)]
+        blocks += [((), (N_UNITS - 2, N_UNITS - 1))]
+        for prep, mult in blocks:
+            for n in prep:
+                transposes(n)
+            if prep:
+                regroup(prep[0])
+                quantise(prep[0], 2 if prep[0] == 0 else 1)
+            if mult[0] == 0:
+                tables()
+            multiply(mult[0])
+            products(mult[0])
+            if prep:
+                regroup(prep[1])
+            plain_out(mult[0])
+            if prep:
+                quantise(prep[1], 1)
+            add_and_store(mult[0])
+            for n in mult[1:]:
+                multiply(n)
+                products(n)
+                plain_out(n)
+                add_and_store(n)

@@ -190,22 +190,20 @@ def tile_mla_pa_t_kernel(tc, x, Wq, Wk, out_0, out_1):
 
         def plain_out(n):
             b, t0 = where(n)
-            dst = out_sb[b][:, :, t0 : t0 + 2, :].rearrange("p q a (h s c) -> p q a h s c", h=2, s=2)
-            nc.scalar.copy(
-                out=dst[:, :, :, :, 0, :],
-                in_=live[("nope", n)][:].rearrange("p (a q h c) -> p q a h c", a=2, q=2, h=2),
-            )
+            nope = live[("nope", n)][:].rearrange("p (a q h c) -> p q a h c", a=2, q=2, h=2)
+            for qk in range(2):
+                dst = out_sb[b][:, qk, t0 : t0 + 2, :].rearrange("p a (h s c) -> p a h s c", h=2, s=2)
+                nc.scalar.copy(out=dst[:, :, :, 0, :], in_=nope[:, qk])
 
         def products(n):
             b, t0 = where(n)
             rope = live[("rope", n)]
-            dst = out_sb[b][:, :, t0 : t0 + 2, :].rearrange("p q a (h s c) -> p q a h s c", h=2, s=2)
-            nc.vector.tensor_tensor(
-                out=dst[:, :, :, :, 1, :],
-                in0=rope[:].rearrange("p (a q h c) -> p q a h c", a=2, q=2, h=2),
-                in1=cos_t[:, t0 : t0 + 2].unsqueeze(1).to_broadcast([P, 2, 2, 2, 2 * NPAIRS]),
-                op=ALU.mult,
-            )
+            rope_c = rope[:].rearrange("p (a q h c) -> p q a h c", a=2, q=2, h=2)
+            for qk in range(2):
+                dst = out_sb[b][:, qk, t0 : t0 + 2, :].rearrange("p a (h s c) -> p a h s c", h=2, s=2)
+                nc.vector.tensor_tensor(
+                    out=dst[:, :, :, 1, :], in0=rope_c[:, qk], in1=cos_t[:, t0 : t0 + 2], op=ALU.mult
+                )
             cross = work.tile([P, 2, 2, 2, 2, NPAIRS], F32, name="cross")
             rope_e = rope[:].rearrange("p (a q h i e) -> p q a h i e", a=2, q=2, h=2, e=2)
             for e in range(2):
@@ -219,14 +217,15 @@ def tile_mla_pa_t_kernel(tc, x, Wq, Wk, out_0, out_1):
 
         def add_and_store(n):
             b, t0 = where(n)
-            rot = out_sb[b][:, :, t0 : t0 + 2, :].rearrange("p q a (h s i e) -> p q (a h) s i e", h=2, s=2, e=2)
             eng = nc.gpsimd if n < GP_ADD_UNTIL else nc.vector
-            eng.tensor_tensor(
-                out=rot[:, :, :, 1],
-                in0=rot[:, :, :, 1],
-                in1=live[("cross", n)][:].rearrange("p e q a h i -> p q (a h) i e"),
-                op=ALU.add,
-            )
+            for qk in range(2):
+                rot = out_sb[b][:, qk, t0 : t0 + 2, :].rearrange("p a (h s i e) -> p (a h) s i e", h=2, s=2, e=2)
+                eng.tensor_tensor(
+                    out=rot[:, :, 1],
+                    in0=rot[:, :, 1],
+                    in1=live[("cross", n)][:, :, qk].rearrange("p e a h i -> p (a h) i e"),
+                    op=ALU.add,
+                )
             if n in stores:
                 sb, st0, snt = stores[n]
                 for qk in range(2):

@@ -87,7 +87,7 @@ def tile_mla_pa_t_kernel(tc, x, Wq, Wk, out_0, out_1):
         half_sq = keep.tile([P, 2, T, NPAIRS], F32, name="half_sq")
         nc.scalar.activation(out=half_sq[:], in_=half_sin[:], func=ACT.Square)
         cos_t = keep.tile([P, T, 2, 2 * NPAIRS], F32, name="cos_t")
-        sin_t = keep.tile([P, 2, T, 2, NPAIRS], F32, name="sin_t")
+        sin_t = keep.tile([P, T, 2, NPAIRS, 2], F32, name="sin_t")
 
         def tables():
             for h in range(2):
@@ -101,7 +101,7 @@ def tile_mla_pa_t_kernel(tc, x, Wq, Wk, out_0, out_1):
                 )
             for e, sign in ((0, -1.0), (1, 1.0)):
                 nc.vector.tensor_scalar(
-                    out=sin_t[:, e],
+                    out=sin_t[:, :, :, :, e],
                     in0=half_sq[:, 1].unsqueeze(2).to_broadcast([P, T, 2, NPAIRS]),
                     scalar1=-2.0 * sign,
                     scalar2=sign,
@@ -127,9 +127,14 @@ def tile_mla_pa_t_kernel(tc, x, Wq, Wk, out_0, out_1):
                 in_=wgrp[:, g].rearrange("p s q h c t -> p (s q h c t)"),
             )
 
-        out_sb = [keep.tile([P, 2, T, 256], F32, name="out_sb%d" % b) for b in range(B)]
-        stores = {1: (0, 0, 4), 3: (0, 4, 4), 5: (1, 0, 4), 7: (1, 4, 4), 9: (2, 0, 4), 11: (2, 4, 4),
-                  13: (3, 0, 4), 14: (3, 4, 2), 15: (3, 6, 2)}
+        groups = [(n, n + 1) for n in range(0, N_UNITS - 2, 2)] + [(N_UNITS - 2,), (N_UNITS - 1,)]
+        out_of = {}
+        last_of = {}
+        for group in groups:
+            og = keep.tile([P, len(group), 2, 512], F32, name="og%d" % group[0])
+            for u, n in enumerate(group):
+                out_of[n] = og[:, u]
+            last_of[group[-1]] = (og, group)
         live = {}
 
         def where(n):
@@ -190,47 +195,51 @@ def tile_mla_pa_t_kernel(tc, x, Wq, Wk, out_0, out_1):
 
         def plain_out(n):
             b, t0 = where(n)
-            nope = live[("nope", n)][:].rearrange("p (a q h c) -> p q a h c", a=2, q=2, h=2)
-            for qk in range(2):
-                dst = out_sb[b][:, qk, t0 : t0 + 2, :].rearrange("p a (h s c) -> p a h s c", h=2, s=2)
-                nc.scalar.copy(out=dst[:, :, :, 0, :], in_=nope[:, qk])
+            dst = out_of[n].rearrange("p q (a h s c) -> p q a h s c", a=2, h=2, s=2)
+            nc.scalar.copy(
+                out=dst[:, :, :, :, 0, :],
+                in_=live[("nope", n)][:].rearrange("p (a q h c) -> p q a h c", a=2, q=2, h=2),
+            )
 
         def products(n):
             b, t0 = where(n)
             rope = live[("rope", n)]
-            rope_c = rope[:].rearrange("p (a q h c) -> p q a h c", a=2, q=2, h=2)
-            for qk in range(2):
-                dst = out_sb[b][:, qk, t0 : t0 + 2, :].rearrange("p a (h s c) -> p a h s c", h=2, s=2)
-                nc.vector.tensor_tensor(
-                    out=dst[:, :, :, 1, :], in0=rope_c[:, qk], in1=cos_t[:, t0 : t0 + 2], op=ALU.mult
-                )
-            cross = work.tile([P, 2, 2, 2, 2, NPAIRS], F32, name="cross")
-            rope_e = rope[:].rearrange("p (a q h i e) -> p q a h i e", a=2, q=2, h=2, e=2)
-            for e in range(2):
-                nc.vector.tensor_tensor(
-                    out=cross[:, e],
-                    in0=rope_e[:, :, :, :, :, 1 - e],
-                    in1=sin_t[:, e, t0 : t0 + 2].unsqueeze(1).to_broadcast([P, 2, 2, 2, NPAIRS]),
-                    op=ALU.mult,
-                )
+            dst = out_of[n].rearrange("p q (a h s c) -> p q a h s c", a=2, h=2, s=2)
+            nc.vector.tensor_tensor(
+                out=dst[:, :, :, :, 1, :],
+                in0=rope[:].rearrange("p (a q h c) -> p q a h c", a=2, q=2, h=2),
+                in1=cos_t[:, t0 : t0 + 2].unsqueeze(1).to_broadcast([P, 2, 2, 2, 2 * NPAIRS]),
+                op=ALU.mult,
+            )
+            cross = work.tile([P, 2, 2, 2 * NPAIRS, 2], F32, name="cross")
+            nc.vector.tensor_tensor(
+                out=cross[:],
+                in0=rope[:].rearrange("p (a q hi e) -> p a q hi e", a=2, q=2, e=2)[:, :, :, :, ::-1],
+                in1=sin_t[:, t0 : t0 + 2]
+                .rearrange("p a h i e -> p a (h i) e")
+                .unsqueeze(2)
+                .to_broadcast([P, 2, 2, 2 * NPAIRS, 2]),
+                op=ALU.mult,
+            )
             live[("cross", n)] = cross
 
         def add_and_store(n):
             b, t0 = where(n)
             eng = nc.gpsimd if n < GP_ADD_UNTIL else nc.vector
-            for qk in range(2):
-                rot = out_sb[b][:, qk, t0 : t0 + 2, :].rearrange("p a (h s i e) -> p (a h) s i e", h=2, s=2, e=2)
-                eng.tensor_tensor(
-                    out=rot[:, :, 1],
-                    in0=rot[:, :, 1],
-                    in1=live[("cross", n)][:, :, qk].rearrange("p e a h i -> p (a h) i e"),
-                    op=ALU.add,
-                )
-            if n in stores:
-                sb, st0, snt = stores[n]
+            rot = out_of[n].rearrange("p q (a h s c) -> p q a h s c", a=2, h=2, s=2)
+            eng.tensor_tensor(
+                out=rot[:, :, :, :, 1, :],
+                in0=rot[:, :, :, :, 1, :],
+                in1=live[("cross", n)][:].rearrange("p a q (h i) e -> p q a h (i e)", h=2),
+                op=ALU.add,
+            )
+            if n in last_of:
+                og, group = last_of[n]
+                gb, gt0 = where(group[0])
                 for qk in range(2):
                     nc.sync.dma_start(
-                        out=out_views[qk][sb][:, st0 : st0 + snt, :], in_=out_sb[sb][:, qk, st0 : st0 + snt, :]
+                        out=out_views[qk][gb][:, gt0 : gt0 + 2 * len(group), :].rearrange("p (u a) d -> p u (a d)", a=2),
+                        in_=og[:, :, qk, :],
                     )
 
         blocks = [((0, 1), (0,)), ((2, 3), (1,))]

@@ -86,28 +86,25 @@ def tile_mla_pa_t_kernel(tc, x, Wq, Wk, out_0, out_1):
         nc.scalar.activation(out=half_sin[:], in_=frac[:], func=ACT.Sin, scale=math.pi)
         half_sq = keep.tile([P, 2, T, NPAIRS], F32, name="half_sq")
         nc.scalar.activation(out=half_sq[:], in_=half_sin[:], func=ACT.Square)
-        cos_t = keep.tile([P, T, 2, 2 * NPAIRS], F32, name="cos_t")
-        sin_t = keep.tile([P, T, 2, NPAIRS, 2], F32, name="sin_t")
-
-        def tables():
-            for h in range(2):
-                nc.vector.tensor_scalar(
-                    out=cos_t[:, :, h, :].rearrange("p t (i e) -> p t i e", e=2),
-                    in0=half_sq[:, 0].unsqueeze(3).to_broadcast([P, T, NPAIRS, 2]),
-                    scalar1=-2.0,
-                    scalar2=1.0,
-                    op0=ALU.mult,
-                    op1=ALU.add,
-                )
-            for e, sign in ((0, -1.0), (1, 1.0)):
-                nc.vector.tensor_scalar(
-                    out=sin_t[:, :, :, :, e],
-                    in0=half_sq[:, 1].unsqueeze(2).to_broadcast([P, T, 2, NPAIRS]),
-                    scalar1=-2.0 * sign,
-                    scalar2=sign,
-                    op0=ALU.mult,
-                    op1=ALU.add,
-                )
+        cos_t = keep.tile([P, T, NPAIRS, 2], F32, name="cos_t")
+        sin_t = keep.tile([P, T, NPAIRS, 2], F32, name="sin_t")
+        plus_one = keep.tile([P, 1], F32, name="plus_one")
+        nc.vector.memset(plus_one[:], 1.0)
+        minus_one = keep.tile([P, 1], F32, name="minus_one")
+        nc.vector.memset(minus_one[:], -1.0)
+        nc.scalar.activation(
+            out=cos_t[:],
+            in_=half_sq[:, 0].unsqueeze(3).to_broadcast([P, T, NPAIRS, 2]),
+            func=ACT.Identity,
+            bias=plus_one[:],
+            scale=-2.0,
+        )
+        nc.scalar.activation(
+            out=sin_t[:, :, :, 0], in_=half_sq[:, 1], func=ACT.Identity, bias=minus_one[:], scale=2.0
+        )
+        nc.scalar.activation(
+            out=sin_t[:, :, :, 1], in_=half_sq[:, 1], func=ACT.Identity, bias=plus_one[:], scale=-2.0
+        )
 
         wgrp = keep.tile([P, 2, 2, 2, 2, 64, 4], BF16, name="wgrp", align_bytes=64)
         wcodes = keep.tile([P, 2, 512], U32, name="wcodes", align_bytes=64)
@@ -127,14 +124,7 @@ def tile_mla_pa_t_kernel(tc, x, Wq, Wk, out_0, out_1):
                 in_=wgrp[:, g].rearrange("p s q h c t -> p (s q h c t)"),
             )
 
-        groups = [(n, n + 1) for n in range(0, N_UNITS - 2, 2)] + [(N_UNITS - 2,), (N_UNITS - 1,)]
-        out_of = {}
-        last_of = {}
-        for group in groups:
-            og = keep.tile([P, len(group), 2, 512], F32, name="og%d" % group[0])
-            for u, n in enumerate(group):
-                out_of[n] = og[:, u]
-            last_of[group[-1]] = (og, group)
+        out_of = [keep.tile([P, 2, 512], F32, name="ou%d" % n) for n in range(N_UNITS)]
         live = {}
 
         def where(n):
@@ -204,43 +194,33 @@ def tile_mla_pa_t_kernel(tc, x, Wq, Wk, out_0, out_1):
         def products(n):
             b, t0 = where(n)
             rope = live[("rope", n)]
-            dst = out_of[n].rearrange("p q (a h s c) -> p q a h s c", a=2, h=2, s=2)
+            pairs = rope[:].rearrange("p (a g i e) -> p a g i e", a=2, g=4, e=2)
+            prod = work.tile([P, 2, 2, 4, NPAIRS, 2], F32, name="prod")
             nc.vector.tensor_tensor(
-                out=dst[:, :, :, :, 1, :],
-                in0=rope[:].rearrange("p (a q h c) -> p q a h c", a=2, q=2, h=2),
-                in1=cos_t[:, t0 : t0 + 2].unsqueeze(1).to_broadcast([P, 2, 2, 2, 2 * NPAIRS]),
+                out=prod[:, 0],
+                in0=pairs,
+                in1=cos_t[:, t0 : t0 + 2].unsqueeze(2).to_broadcast([P, 2, 4, NPAIRS, 2]),
                 op=ALU.mult,
             )
-            cross = work.tile([P, 2, 2, 2 * NPAIRS, 2], F32, name="cross")
             nc.vector.tensor_tensor(
-                out=cross[:],
-                in0=rope[:].rearrange("p (a q hi e) -> p a q hi e", a=2, q=2, e=2)[:, :, :, :, ::-1],
-                in1=sin_t[:, t0 : t0 + 2]
-                .rearrange("p a h i e -> p a (h i) e")
-                .unsqueeze(2)
-                .to_broadcast([P, 2, 2, 2 * NPAIRS, 2]),
+                out=prod[:, 1],
+                in0=pairs[:, :, :, :, ::-1],
+                in1=sin_t[:, t0 : t0 + 2].unsqueeze(2).to_broadcast([P, 2, 4, NPAIRS, 2]),
                 op=ALU.mult,
             )
-            live[("cross", n)] = cross
+            live[("prod", n)] = prod
 
         def add_and_store(n):
             b, t0 = where(n)
             eng = nc.gpsimd if n < GP_ADD_UNTIL else nc.vector
             rot = out_of[n].rearrange("p q (a h s c) -> p q a h s c", a=2, h=2, s=2)
-            eng.tensor_tensor(
-                out=rot[:, :, :, :, 1, :],
-                in0=rot[:, :, :, :, 1, :],
-                in1=live[("cross", n)][:].rearrange("p a q (h i) e -> p q a h (i e)", h=2),
-                op=ALU.add,
-            )
-            if n in last_of:
-                og, group = last_of[n]
-                gb, gt0 = where(group[0])
-                for qk in range(2):
-                    nc.sync.dma_start(
-                        out=out_views[qk][gb][:, gt0 : gt0 + 2 * len(group), :].rearrange("p (u a) d -> p u (a d)", a=2),
-                        in_=og[:, :, qk, :],
-                    )
+            prod = live[("prod", n)][:].rearrange("p k a (q h) i e -> p k q a h (i e)", q=2)
+            eng.tensor_tensor(out=rot[:, :, :, :, 1, :], in0=prod[:, 0], in1=prod[:, 1], op=ALU.add)
+            for qk in range(2):
+                nc.sync.dma_start(
+                    out=out_views[qk][b][:, t0 : t0 + 2, :],
+                    in_=out_of[n][:, qk, :].rearrange("p (a d) -> p a d", a=2),
+                )
 
         blocks = [((0, 1), (0,)), ((2, 3), (1,))]
         blocks += [((n + 2, n + 3), (n, n + 1)) for n in range(2, N_UNITS - 2, 2)]
@@ -251,8 +231,6 @@ def tile_mla_pa_t_kernel(tc, x, Wq, Wk, out_0, out_1):
             if prep:
                 regroup(prep[0])
                 quantise(prep[0], 2 if prep[0] == 0 else 1)
-            if mult[0] == 0:
-                tables()
             multiply(mult[0])
             products(mult[0])
             if prep:

@@ -34,6 +34,7 @@ def tile_mla_pa_t_kernel(tc, x, Wq, Wk, out_0, out_1):
         ctx.enter_context(tc.manual_schedule())
         keep = ctx.enter_context(tc.tile_pool(name="keep", bufs=1))
         work = ctx.enter_context(tc.tile_pool(name="work", bufs=4))
+        mxin = ctx.enter_context(tc.tile_pool(name="mxin", bufs=3))
         ps_t = ctx.enter_context(tc.psum_pool(name="ps_t", bufs=4))
         ps_r = ctx.enter_context(tc.psum_pool(name="ps_r", bufs=2))
         ps_n = ctx.enter_context(tc.psum_pool(name="ps_n", bufs=2))
@@ -141,36 +142,34 @@ def tile_mla_pa_t_kernel(tc, x, Wq, Wk, out_0, out_1):
                 live[("xt", n, a)] = xt
 
         def regroup(n):
-            grp = work.tile([P, 2, 2, P, 4], BF16, name="grp", align_bytes=64)
-            grp_words = grp[:].bitcast(F32)
+            if n % 2 == 0:
+                live[("grp", n // 2)] = mxin.tile([P, 4, 2, P, 4], BF16, name="grp", align_bytes=64)
+                live[("codes", n // 2)] = mxin.tile([P, 1024], U32, name="codes", align_bytes=64)
+                live[("scales", n // 2)] = mxin.tile([P, 1024], U8, name="scales", align_bytes=64)
+            grp_words = live[("grp", n // 2)][:].bitcast(F32)
             for a in range(2):
                 nc.scalar.copy(
-                    out=grp_words[:, a], in_=live[("xt", n, a)][:].rearrange("p (g u) r -> p g r u", u=2)
+                    out=grp_words[:, 2 * (n % 2) + a],
+                    in_=live[("xt", n, a)][:].rearrange("p (g u) r -> p g r u", u=2),
                 )
-            live[("grp", n)] = grp
 
-        def quantise(n, pieces):
-            grp = live[("grp", n)][:].rearrange("p a g r t -> p (a g r t)")
-            codes = work.tile([P, 512], U32, name="codes", align_bytes=64)
-            scales = work.tile([P, 512], U8, name="scales", align_bytes=64)
-            width = 512 // pieces
-            for piece in range(pieces):
-                cols = slice(piece * width, (piece + 1) * width)
-                nc.vector.quantize_mx(
-                    out=codes[:, cols].bitcast(FP8X4),
-                    scales=scales[:, cols],
-                    in_=grp[:, 4 * piece * width : 4 * (piece + 1) * width],
-                )
-            live[("q", n)] = (codes, scales)
+        def quantise(block, first_tile, tiles):
+            grp = live[("grp", block)][:].rearrange("p a g r t -> p (a g r t)")
+            cols = slice(256 * first_tile, 256 * (first_tile + tiles))
+            nc.vector.quantize_mx(
+                out=live[("codes", block)][:, cols].bitcast(FP8X4),
+                scales=live[("scales", block)][:, cols],
+                in_=grp[:, 1024 * first_tile : 1024 * (first_tile + tiles)],
+            )
 
         def multiply(n):
-            codes, scales = live[("q", n)]
+            codes, scales = live[("codes", n // 2)], live[("scales", n // 2)]
             rope = ps_r.tile([P, 512], F32, name="rope")
             nope = ps_n.tile([P, 512], F32, name="nope")
             for s, bank in ((ROPE, rope), (NOPE, nope)):
                 for a in range(2):
                     for g in range(2):
-                        col = (2 * a + g) * P
+                        col = (2 * (2 * (n % 2) + a) + g) * P
                         nc.tensor.matmul_mx(
                             out=bank[:, 256 * a : 256 * a + 256],
                             lhsT=codes[:, col : col + P].bitcast(FP8X4),
@@ -194,17 +193,18 @@ def tile_mla_pa_t_kernel(tc, x, Wq, Wk, out_0, out_1):
         def products(n):
             b, t0 = where(n)
             rope = live[("rope", n)]
-            pairs = rope[:].rearrange("p (a g i e) -> p a g i e", a=2, g=4, e=2)
-            prod = work.tile([P, 2, 2, 4, NPAIRS, 2], F32, name="prod")
+            prod = work.tile([P, 2, 2, 2, 2, NPAIRS, 2], F32, name="prod")
+            prod_banked = prod[:].rearrange("p k q a h i e -> p k a q h i e")
+            pairs = rope[:].rearrange("p (a q h i e) -> p a q h i e", a=2, q=2, h=2, e=2)
             nc.vector.tensor_tensor(
-                out=prod[:, 0],
+                out=prod_banked[:, 0],
                 in0=pairs,
                 in1=cos_t[:, t0 : t0 + 2].unsqueeze(2).to_broadcast([P, 2, 4, NPAIRS, 2]),
                 op=ALU.mult,
             )
             nc.vector.tensor_tensor(
-                out=prod[:, 1],
-                in0=pairs[:, :, :, :, ::-1],
+                out=prod_banked[:, 1],
+                in0=pairs[:, :, :, :, :, ::-1],
                 in1=sin_t[:, t0 : t0 + 2].unsqueeze(2).to_broadcast([P, 2, 4, NPAIRS, 2]),
                 op=ALU.mult,
             )
@@ -214,7 +214,7 @@ def tile_mla_pa_t_kernel(tc, x, Wq, Wk, out_0, out_1):
             b, t0 = where(n)
             eng = nc.gpsimd if n < GP_ADD_UNTIL else nc.vector
             rot = out_of[n].rearrange("p q (a h s c) -> p q a h s c", a=2, h=2, s=2)
-            prod = live[("prod", n)][:].rearrange("p k a (q h) i e -> p k q a h (i e)", q=2)
+            prod = live[("prod", n)][:].rearrange("p k q a h i e -> p k q a h (i e)")
             eng.tensor_tensor(out=rot[:, :, :, :, 1, :], in0=prod[:, 0], in1=prod[:, 1], op=ALU.add)
             for qk in range(2):
                 nc.sync.dma_start(
@@ -222,25 +222,29 @@ def tile_mla_pa_t_kernel(tc, x, Wq, Wk, out_0, out_1):
                     in_=out_of[n][:, qk, :].rearrange("p (a d) -> p a d", a=2),
                 )
 
-        blocks = [((0, 1), (0,)), ((2, 3), (1,))]
-        blocks += [((n + 2, n + 3), (n, n + 1)) for n in range(2, N_UNITS - 2, 2)]
-        blocks += [((), (N_UNITS - 2, N_UNITS - 1))]
-        for prep, mult in blocks:
-            for n in prep:
-                transposes(n)
-            if prep:
-                regroup(prep[0])
-                quantise(prep[0], 2 if prep[0] == 0 else 1)
-            multiply(mult[0])
-            products(mult[0])
-            if prep:
-                regroup(prep[1])
-            plain_out(mult[0])
-            if prep:
-                quantise(prep[1], 1)
-            add_and_store(mult[0])
-            for n in mult[1:]:
-                multiply(n)
-                products(n)
-                plain_out(n)
-                add_and_store(n)
+        def finish(n):
+            multiply(n)
+            products(n)
+            plain_out(n)
+            add_and_store(n)
+
+        transposes(0)
+        transposes(1)
+        regroup(0)
+        quantise(0, 0, 1)
+        quantise(0, 1, 1)
+        regroup(1)
+        finish(0)
+        quantise(0, 2, 2)
+        for block in range(1, N_UNITS // 2 + 1):
+            ahead = block < N_UNITS // 2
+            if ahead:
+                transposes(2 * block)
+                transposes(2 * block + 1)
+                regroup(2 * block)
+                regroup(2 * block + 1)
+            if block > 1:
+                finish(2 * block - 2)
+            if ahead:
+                quantise(block, 0, 4)
+            finish(2 * block - 1)

@@ -34,7 +34,6 @@ def tile_mla_pa_t_kernel(tc, x, Wq, Wk, out_0, out_1):
         ctx.enter_context(tc.manual_schedule())
         keep = ctx.enter_context(tc.tile_pool(name="keep", bufs=1))
         work = ctx.enter_context(tc.tile_pool(name="work", bufs=4))
-        mxin = ctx.enter_context(tc.tile_pool(name="mxin", bufs=3))
         ps_t = ctx.enter_context(tc.psum_pool(name="ps_t", bufs=4))
         ps_r = ctx.enter_context(tc.psum_pool(name="ps_r", bufs=2))
         ps_n = ctx.enter_context(tc.psum_pool(name="ps_n", bufs=2))
@@ -45,17 +44,25 @@ def tile_mla_pa_t_kernel(tc, x, Wq, Wk, out_0, out_1):
         chunks = [(0, 0, 1), (0, 1, 1), (0, 2, 2), (0, 4, 2), (0, 6, 2), (1, 0, 4), (1, 4, 4), (2, 0, 8), (3, 0, 8)]
         x_words = {}
         wraw = keep.tile([P, 2, 8, 256], BF16, name="wraw")
-        for g in range(2):
+
+        def load_w(g):
             for qk, w_dram in enumerate((Wq, Wk)):
                 nc.sync.dma_start(
                     out=wraw[:, qk, 4 * g : 4 * g + 4, :].rearrange("p (u e) c -> p u e c", e=2),
                     in_=w_dram.rearrange("(j q e) c -> q j e c", j=4, e=2)[:, 2 * g : 2 * g + 2],
                 )
-        for b, t0, nt in chunks:
+
+        def load_x(b, t0, nt):
             xs = keep.tile([P, nt, DIM], BF16, name="x%d_%d" % (b, t0))
             nc.sync.dma_start(out=xs[:], in_=x_view[b][:, t0 : t0 + nt, :])
             for t in range(nt):
                 x_words[(b, t0 + t)] = xs[:, t, :].bitcast(F32)
+
+        load_w(0)
+        load_x(*chunks[0])
+        load_w(1)
+        for chunk in chunks[1:]:
+            load_x(*chunk)
 
         zero = keep.tile([P, 1], F32, name="zero")
         nc.vector.memset(zero[:], 0.0)
@@ -87,25 +94,28 @@ def tile_mla_pa_t_kernel(tc, x, Wq, Wk, out_0, out_1):
         nc.scalar.activation(out=half_sin[:], in_=frac[:], func=ACT.Sin, scale=math.pi)
         half_sq = keep.tile([P, 2, T, NPAIRS], F32, name="half_sq")
         nc.scalar.activation(out=half_sq[:], in_=half_sin[:], func=ACT.Square)
-        cos_t = keep.tile([P, T, NPAIRS, 2], F32, name="cos_t")
-        sin_t = keep.tile([P, T, NPAIRS, 2], F32, name="sin_t")
-        plus_one = keep.tile([P, 1], F32, name="plus_one")
-        nc.vector.memset(plus_one[:], 1.0)
-        minus_one = keep.tile([P, 1], F32, name="minus_one")
-        nc.vector.memset(minus_one[:], -1.0)
-        nc.scalar.activation(
-            out=cos_t[:],
-            in_=half_sq[:, 0].unsqueeze(3).to_broadcast([P, T, NPAIRS, 2]),
-            func=ACT.Identity,
-            bias=plus_one[:],
-            scale=-2.0,
-        )
-        nc.scalar.activation(
-            out=sin_t[:, :, :, 0], in_=half_sq[:, 1], func=ACT.Identity, bias=minus_one[:], scale=2.0
-        )
-        nc.scalar.activation(
-            out=sin_t[:, :, :, 1], in_=half_sq[:, 1], func=ACT.Identity, bias=plus_one[:], scale=-2.0
-        )
+        cos_t = keep.tile([P, T, 2, 2 * NPAIRS], F32, name="cos_t")
+        sin_t = keep.tile([P, T, 2, NPAIRS, 2], F32, name="sin_t")
+
+        def tables():
+            for h in range(2):
+                nc.vector.tensor_scalar(
+                    out=cos_t[:, :, h, :].rearrange("p t (i e) -> p t i e", e=2),
+                    in0=half_sq[:, 0].unsqueeze(3).to_broadcast([P, T, NPAIRS, 2]),
+                    scalar1=-2.0,
+                    scalar2=1.0,
+                    op0=ALU.mult,
+                    op1=ALU.add,
+                )
+            for e, sign in ((0, -1.0), (1, 1.0)):
+                nc.vector.tensor_scalar(
+                    out=sin_t[:, :, :, :, e],
+                    in0=half_sq[:, 1].unsqueeze(2).to_broadcast([P, T, 2, NPAIRS]),
+                    scalar1=-2.0 * sign,
+                    scalar2=sign,
+                    op0=ALU.mult,
+                    op1=ALU.add,
+                )
 
         wgrp = keep.tile([P, 2, 2, 2, 2, 64, 4], BF16, name="wgrp", align_bytes=64)
         wcodes = keep.tile([P, 2, 512], U32, name="wcodes", align_bytes=64)
@@ -118,14 +128,24 @@ def tile_mla_pa_t_kernel(tc, x, Wq, Wk, out_0, out_1):
                     if (g, s, qk) in S_REGROUP:
                         nc.scalar.copy(out=wgrp[:, g, s, qk], in_=permuted)
                     else:
-                        nc.vector.tensor_copy(out=wgrp[:, g, s, qk], in_=permuted)
+                        nc.vector.tensor_copy(
+                            out=wgrp[:, g, s, qk].rearrange("p h (c i) t -> p h c t i", i=4),
+                            in_=src[:, :, :, 1 - s, :].rearrange("p t h (c i) -> p h c t i", i=4),
+                        )
             nc.vector.quantize_mx(
                 out=wcodes[:, g, :].bitcast(FP8X4),
                 scales=wscales[:, g, :],
                 in_=wgrp[:, g].rearrange("p s q h c t -> p (s q h c t)"),
             )
 
-        out_of = [keep.tile([P, 2, 512], F32, name="ou%d" % n) for n in range(N_UNITS)]
+        groups = [(n, n + 1) for n in range(0, N_UNITS - 2, 2)] + [(N_UNITS - 2,), (N_UNITS - 1,)]
+        out_of = {}
+        last_of = {}
+        for group in groups:
+            og = keep.tile([P, len(group), 2, 512], F32, name="og%d" % group[0])
+            for u, n in enumerate(group):
+                out_of[n] = og[:, u]
+            last_of[group[-1]] = (og, group)
         live = {}
 
         def where(n):
@@ -142,34 +162,36 @@ def tile_mla_pa_t_kernel(tc, x, Wq, Wk, out_0, out_1):
                 live[("xt", n, a)] = xt
 
         def regroup(n):
-            if n % 2 == 0:
-                live[("grp", n // 2)] = mxin.tile([P, 4, 2, P, 4], BF16, name="grp", align_bytes=64)
-                live[("codes", n // 2)] = mxin.tile([P, 1024], U32, name="codes", align_bytes=64)
-                live[("scales", n // 2)] = mxin.tile([P, 1024], U8, name="scales", align_bytes=64)
-            grp_words = live[("grp", n // 2)][:].bitcast(F32)
+            grp = work.tile([P, 2, 2, P, 4], BF16, name="grp", align_bytes=64)
+            grp_words = grp[:].bitcast(F32)
             for a in range(2):
                 nc.scalar.copy(
-                    out=grp_words[:, 2 * (n % 2) + a],
-                    in_=live[("xt", n, a)][:].rearrange("p (g u) r -> p g r u", u=2),
+                    out=grp_words[:, a], in_=live[("xt", n, a)][:].rearrange("p (g u) r -> p g r u", u=2)
                 )
+            live[("grp", n)] = grp
 
-        def quantise(block, first_tile, tiles):
-            grp = live[("grp", block)][:].rearrange("p a g r t -> p (a g r t)")
-            cols = slice(256 * first_tile, 256 * (first_tile + tiles))
-            nc.vector.quantize_mx(
-                out=live[("codes", block)][:, cols].bitcast(FP8X4),
-                scales=live[("scales", block)][:, cols],
-                in_=grp[:, 1024 * first_tile : 1024 * (first_tile + tiles)],
-            )
+        def quantise(n, pieces):
+            grp = live[("grp", n)][:].rearrange("p a g r t -> p (a g r t)")
+            codes = work.tile([P, 512], U32, name="codes", align_bytes=64)
+            scales = work.tile([P, 512], U8, name="scales", align_bytes=64)
+            width = 512 // pieces
+            for piece in range(pieces):
+                cols = slice(piece * width, (piece + 1) * width)
+                nc.vector.quantize_mx(
+                    out=codes[:, cols].bitcast(FP8X4),
+                    scales=scales[:, cols],
+                    in_=grp[:, 4 * piece * width : 4 * (piece + 1) * width],
+                )
+            live[("q", n)] = (codes, scales)
 
         def multiply(n):
-            codes, scales = live[("codes", n // 2)], live[("scales", n // 2)]
+            codes, scales = live[("q", n)]
             rope = ps_r.tile([P, 512], F32, name="rope")
             nope = ps_n.tile([P, 512], F32, name="nope")
             for s, bank in ((ROPE, rope), (NOPE, nope)):
                 for a in range(2):
                     for g in range(2):
-                        col = (2 * (2 * (n % 2) + a) + g) * P
+                        col = (2 * a + g) * P
                         nc.tensor.matmul_mx(
                             out=bank[:, 256 * a : 256 * a + 256],
                             lhsT=codes[:, col : col + P].bitcast(FP8X4),
@@ -193,58 +215,67 @@ def tile_mla_pa_t_kernel(tc, x, Wq, Wk, out_0, out_1):
         def products(n):
             b, t0 = where(n)
             rope = live[("rope", n)]
-            prod = work.tile([P, 2, 2, 2, 2, NPAIRS, 2], F32, name="prod")
-            prod_banked = prod[:].rearrange("p k q a h i e -> p k a q h i e")
-            pairs = rope[:].rearrange("p (a q h i e) -> p a q h i e", a=2, q=2, h=2, e=2)
+            dst = out_of[n].rearrange("p q (a h s c) -> p q a h s c", a=2, h=2, s=2)
             nc.vector.tensor_tensor(
-                out=prod_banked[:, 0],
-                in0=pairs,
-                in1=cos_t[:, t0 : t0 + 2].unsqueeze(2).to_broadcast([P, 2, 4, NPAIRS, 2]),
+                out=dst[:, :, :, :, 1, :],
+                in0=rope[:].rearrange("p (a q h c) -> p q a h c", a=2, q=2, h=2),
+                in1=cos_t[:, t0 : t0 + 2].unsqueeze(1).to_broadcast([P, 2, 2, 2, 2 * NPAIRS]),
                 op=ALU.mult,
             )
+            cross = work.tile([P, 2, 2, 2 * NPAIRS, 2], F32, name="cross")
             nc.vector.tensor_tensor(
-                out=prod_banked[:, 1],
-                in0=pairs[:, :, :, :, :, ::-1],
-                in1=sin_t[:, t0 : t0 + 2].unsqueeze(2).to_broadcast([P, 2, 4, NPAIRS, 2]),
+                out=cross[:],
+                in0=rope[:].rearrange("p (a q hi e) -> p a q hi e", a=2, q=2, e=2)[:, :, :, :, ::-1],
+                in1=sin_t[:, t0 : t0 + 2]
+                .rearrange("p a h i e -> p a (h i) e")
+                .unsqueeze(2)
+                .to_broadcast([P, 2, 2, 2 * NPAIRS, 2]),
                 op=ALU.mult,
             )
-            live[("prod", n)] = prod
+            live[("cross", n)] = cross
 
         def add_and_store(n):
             b, t0 = where(n)
             eng = nc.gpsimd if n < GP_ADD_UNTIL else nc.vector
             rot = out_of[n].rearrange("p q (a h s c) -> p q a h s c", a=2, h=2, s=2)
-            prod = live[("prod", n)][:].rearrange("p k q a h i e -> p k q a h (i e)")
-            eng.tensor_tensor(out=rot[:, :, :, :, 1, :], in0=prod[:, 0], in1=prod[:, 1], op=ALU.add)
-            for qk in range(2):
-                nc.sync.dma_start(
-                    out=out_views[qk][b][:, t0 : t0 + 2, :],
-                    in_=out_of[n][:, qk, :].rearrange("p (a d) -> p a d", a=2),
-                )
+            eng.tensor_tensor(
+                out=rot[:, :, :, :, 1, :],
+                in0=rot[:, :, :, :, 1, :],
+                in1=live[("cross", n)][:].rearrange("p a q (h i) e -> p q a h (i e)", h=2),
+                op=ALU.add,
+            )
+            if n in last_of:
+                og, group = last_of[n]
+                gb, gt0 = where(group[0])
+                for qk in range(2):
+                    nc.sync.dma_start(
+                        out=out_views[qk][gb][:, gt0 : gt0 + 2 * len(group), :].rearrange("p (u a) d -> p u (a d)", a=2),
+                        in_=og[:, :, qk, :],
+                    )
 
-        def finish(n):
-            multiply(n)
-            products(n)
-            plain_out(n)
-            add_and_store(n)
-
-        transposes(0)
-        transposes(1)
-        regroup(0)
-        quantise(0, 0, 1)
-        quantise(0, 1, 1)
-        regroup(1)
-        finish(0)
-        quantise(0, 2, 2)
-        for block in range(1, N_UNITS // 2 + 1):
-            ahead = block < N_UNITS // 2
-            if ahead:
-                transposes(2 * block)
-                transposes(2 * block + 1)
-                regroup(2 * block)
-                regroup(2 * block + 1)
-            if block > 1:
-                finish(2 * block - 2)
-            if ahead:
-                quantise(block, 0, 4)
-            finish(2 * block - 1)
+        blocks = [((0, 1), (0,)), ((2, 3), (1,))]
+        blocks += [((n + 2, n + 3), (n, n + 1)) for n in range(2, N_UNITS - 2, 2)]
+        blocks += [((), (N_UNITS - 2, N_UNITS - 1))]
+        for prep, mult in blocks:
+            for n in prep:
+                transposes(n)
+            if prep:
+                regroup(prep[0])
+                quantise(prep[0], 2 if prep[0] == 0 else 1)
+            if mult[0] == 0:
+                regroup(prep[1])
+                quantise(prep[1], 1)
+                tables()
+            multiply(mult[0])
+            products(mult[0])
+            if prep and mult[0] > 0:
+                regroup(prep[1])
+            plain_out(mult[0])
+            if prep and mult[0] > 0:
+                quantise(prep[1], 1)
+            add_and_store(mult[0])
+            for n in mult[1:]:
+                multiply(n)
+                products(n)
+                plain_out(n)
+                add_and_store(n)

@@ -44,25 +44,17 @@ def tile_mla_pa_t_kernel(tc, x, Wq, Wk, out_0, out_1):
         chunks = [(0, 0, 1), (0, 1, 1), (0, 2, 2), (0, 4, 2), (0, 6, 2), (1, 0, 4), (1, 4, 4), (2, 0, 8), (3, 0, 8)]
         x_words = {}
         wraw = keep.tile([P, 2, 8, 256], BF16, name="wraw")
-
-        def load_w(g):
+        for g in range(2):
             for qk, w_dram in enumerate((Wq, Wk)):
                 nc.sync.dma_start(
                     out=wraw[:, qk, 4 * g : 4 * g + 4, :].rearrange("p (u e) c -> p u e c", e=2),
                     in_=w_dram.rearrange("(j q e) c -> q j e c", j=4, e=2)[:, 2 * g : 2 * g + 2],
                 )
-
-        def load_x(b, t0, nt):
+        for b, t0, nt in chunks:
             xs = keep.tile([P, nt, DIM], BF16, name="x%d_%d" % (b, t0))
             nc.sync.dma_start(out=xs[:], in_=x_view[b][:, t0 : t0 + nt, :])
             for t in range(nt):
                 x_words[(b, t0 + t)] = xs[:, t, :].bitcast(F32)
-
-        load_w(0)
-        load_x(*chunks[0])
-        load_w(1)
-        for chunk in chunks[1:]:
-            load_x(*chunk)
 
         zero = keep.tile([P, 1], F32, name="zero")
         nc.vector.memset(zero[:], 0.0)
@@ -128,10 +120,7 @@ def tile_mla_pa_t_kernel(tc, x, Wq, Wk, out_0, out_1):
                     if (g, s, qk) in S_REGROUP:
                         nc.scalar.copy(out=wgrp[:, g, s, qk], in_=permuted)
                     else:
-                        nc.vector.tensor_copy(
-                            out=wgrp[:, g, s, qk].rearrange("p h (c i) t -> p h c t i", i=4),
-                            in_=src[:, :, :, 1 - s, :].rearrange("p t h (c i) -> p h c t i", i=4),
-                        )
+                        nc.vector.tensor_copy(out=wgrp[:, g, s, qk], in_=permuted)
             nc.vector.quantize_mx(
                 out=wcodes[:, g, :].bitcast(FP8X4),
                 scales=wscales[:, g, :],
@@ -253,29 +242,23 @@ def tile_mla_pa_t_kernel(tc, x, Wq, Wk, out_0, out_1):
                         in_=og[:, :, qk, :],
                     )
 
-        blocks = [((0, 1), (0,)), ((2, 3), (1,))]
-        blocks += [((n + 2, n + 3), (n, n + 1)) for n in range(2, N_UNITS - 2, 2)]
-        blocks += [((), (N_UNITS - 2, N_UNITS - 1))]
-        for prep, mult in blocks:
-            for n in prep:
-                transposes(n)
-            if prep:
-                regroup(prep[0])
-                quantise(prep[0], 2 if prep[0] == 0 else 1)
-            if mult[0] == 0:
-                regroup(prep[1])
-                quantise(prep[1], 1)
-                tables()
-            multiply(mult[0])
-            products(mult[0])
-            if prep and mult[0] > 0:
-                regroup(prep[1])
-            plain_out(mult[0])
-            if prep and mult[0] > 0:
-                quantise(prep[1], 1)
-            add_and_store(mult[0])
-            for n in mult[1:]:
-                multiply(n)
-                products(n)
-                plain_out(n)
-                add_and_store(n)
+        def prepare(n, pieces):
+            transposes(n)
+            regroup(n)
+            quantise(n, pieces)
+
+        def finish(n):
+            multiply(n)
+            products(n)
+            plain_out(n)
+            add_and_store(n)
+
+        prepare(0, 2)
+        prepare(1, 1)
+        tables()
+        finish(0)
+        prepare(2, 1)
+        for n in range(1, N_UNITS):
+            if n + 2 < N_UNITS:
+                prepare(n + 2, 1)
+            finish(n)

import math
from contextlib import ExitStack

import concourse.mybir as mybir
from concourse.masks import make_identity

F32 = mybir.dt.float32
BF16 = mybir.dt.bfloat16
I32 = mybir.dt.int32
U32 = mybir.dt.uint32
U8 = mybir.dt.uint8
FP8X4 = mybir.dt.float8_e4m3fn_x4
ALU = mybir.AluOpType
ACT = mybir.ActivationFunctionType

P = 128
B = 4
T = 8
DIM = 1024
NPAIRS = 32
RATIO = 10000.0 ** (-1.0 / 32.0)
ROPE = 0
NOPE = 1
FLOPS = 2 * 4096 * 1024 * 512

N_UNITS = 16
GP_ADD_UNTIL = 15
S_REGROUP = ((1, 1, 0), (1, 1, 1))


def tile_mla_pa_t_kernel(tc, x, Wq, Wk, out_0, out_1):
    nc = tc.nc
    with ExitStack() as ctx:
        ctx.enter_context(tc.manual_schedule())
        keep = ctx.enter_context(tc.tile_pool(name="keep", bufs=1))
        work = ctx.enter_context(tc.tile_pool(name="work", bufs=4))
        ps_t = ctx.enter_context(tc.psum_pool(name="ps_t", bufs=4))
        ps_r = ctx.enter_context(tc.psum_pool(name="ps_r", bufs=2))
        ps_n = ctx.enter_context(tc.psum_pool(name="ps_n", bufs=2))

        x_view = x.rearrange("b (p t) k -> b p t k", t=T)
        out_views = [o.rearrange("b (p t) h d -> b p t (h d)", t=T) for o in (out_0, out_1)]

        chunks = [(0, 0, 1), (0, 1, 1), (0, 2, 2), (0, 4, 2), (0, 6, 2), (1, 0, 4), (1, 4, 4), (2, 0, 8), (3, 0, 8)]
        x_words = {}
        wraw = keep.tile([P, 2, 8, 256], BF16, name="wraw")
        for g in range(2):
            for qk, w_dram in enumerate((Wq, Wk)):
                nc.sync.dma_start(
                    out=wraw[:, qk, 4 * g : 4 * g + 4, :].rearrange("p (u e) c -> p u e c", e=2),
                    in_=w_dram.rearrange("(j q e) c -> q j e c", j=4, e=2)[:, 2 * g : 2 * g + 2],
                )
        for b, t0, nt in chunks:
            xs = keep.tile([P, nt, DIM], BF16, name="x%d_%d" % (b, t0))
            nc.sync.dma_start(out=xs[:], in_=x_view[b][:, t0 : t0 + nt, :])
            for t in range(nt):
                x_words[(b, t0 + t)] = xs[:, t, :].bitcast(F32)

        zero = keep.tile([P, 1], F32, name="zero")
        nc.vector.memset(zero[:], 0.0)
        warm = keep.tile([P, 1], F32, name="warm")
        nc.scalar.activation(out=warm[:], in_=zero[:], func=ACT.Sin)
        pos_i = keep.tile([P, T], I32, name="pos_i")
        nc.gpsimd.iota(pos_i[:], pattern=[[1, T]], base=0, channel_multiplier=T)
        ident = keep.tile([P, P], F32, name="ident")
        make_identity(nc, ident[:])

        turns = keep.tile([P, T, NPAIRS], F32, name="turns")
        nc.vector.tensor_scalar(
            out=turns[:, :, 0:1], in0=pos_i[:].unsqueeze(2), scalar1=1.0 / (2.0 * math.pi), scalar2=None, op0=ALU.mult
        )
        for level in range(5):
            w = 1 << level
            nc.vector.tensor_scalar(
                out=turns[:, :, w : 2 * w], in0=turns[:, :, 0:w], scalar1=RATIO**w, scalar2=None, op0=ALU.mult
            )
        whole = keep.tile([P, 2, T, NPAIRS], I32, name="whole")
        nc.vector.tensor_scalar(out=whole[:, 0], in0=turns[:], scalar1=0.25, scalar2=None, op0=ALU.add)
        nc.vector.tensor_copy(out=whole[:, 1], in_=turns[:])
        frac = keep.tile([P, 2, T, NPAIRS], F32, name="frac")
        nc.vector.tensor_tensor(out=frac[:, 0], in0=whole[:, 0], in1=turns[:], op=ALU.subtract)
        nc.vector.scalar_tensor_tensor(
            out=frac[:, 1], in0=whole[:, 1], scalar=0.25, in1=turns[:], op0=ALU.add, op1=ALU.subtract
        )
        half_sin = keep.tile([P, 2, T, NPAIRS], F32, name="half_sin")
        nc.scalar.activation(out=half_sin[:], in_=frac[:], func=ACT.Sin, scale=math.pi)
        half_sq = keep.tile([P, 2, T, NPAIRS], F32, name="half_sq")
        nc.scalar.activation(out=half_sq[:], in_=half_sin[:], func=ACT.Square)
        cos_t = keep.tile([P, T, 2, 2 * NPAIRS], F32, name="cos_t")
        sin_t = keep.tile([P, T, 2, NPAIRS, 2], F32, name="sin_t")

        def tables():
            for h in range(2):
                nc.vector.tensor_scalar(
                    out=cos_t[:, :, h, :].rearrange("p t (i e) -> p t i e", e=2),
                    in0=half_sq[:, 0].unsqueeze(3).to_broadcast([P, T, NPAIRS, 2]),
                    scalar1=-2.0,
                    scalar2=1.0,
                    op0=ALU.mult,
                    op1=ALU.add,
                )
            for e, sign in ((0, -1.0), (1, 1.0)):
                nc.vector.tensor_scalar(
                    out=sin_t[:, :, :, :, e],
                    in0=half_sq[:, 1].unsqueeze(2).to_broadcast([P, T, 2, NPAIRS]),
                    scalar1=-2.0 * sign,
                    scalar2=sign,
                    op0=ALU.mult,
                    op1=ALU.add,
                )

        wgrp = keep.tile([P, 2, 2, 2, 2, 64, 4], BF16, name="wgrp", align_bytes=64)
        wcodes = keep.tile([P, 2, 512], U32, name="wcodes", align_bytes=64)
        wscales = keep.tile([P, 2, 512], U8, name="wscales", align_bytes=64)
        for g in range(2):
            for s in (ROPE, NOPE):
                for qk in range(2):
                    src = wraw[:, qk, 4 * g : 4 * g + 4, :].rearrange("p t (h s c) -> p t h s c", h=2, s=2)
                    permuted = src[:, :, :, 1 - s, :].rearrange("p t h c -> p h c t")
                    if (g, s, qk) in S_REGROUP:
                        nc.scalar.copy(out=wgrp[:, g, s, qk], in_=permuted)
                    else:
                        nc.vector.tensor_copy(out=wgrp[:, g, s, qk], in_=permuted)
            nc.vector.quantize_mx(
                out=wcodes[:, g, :].bitcast(FP8X4),
                scales=wscales[:, g, :],
                in_=wgrp[:, g].rearrange("p s q h c t -> p (s q h c t)"),
            )

        groups = [(n, n + 1) for n in range(0, N_UNITS - 2, 2)] + [(N_UNITS - 2,), (N_UNITS - 1,)]
        out_of = {}
        last_of = {}
        for group in groups:
            og = keep.tile([P, len(group), 2, 512], F32, name="og%d" % group[0])
            for u, n in enumerate(group):
                out_of[n] = og[:, u]
            last_of[group[-1]] = (og, group)
        live = {}

        def where(n):
            return n // 4, 2 * (n % 4)

        def transposes(n):
            b, t0 = where(n)
            for a in range(2):
                xt = ps_t.tile([P, 4, P], F32, name="xt")
                for j in range(4):
                    nc.tensor.transpose(
                        out=xt[:, j, :], in_=x_words[(b, t0 + a)][:, P * j : P * (j + 1)], identity=ident[:]
                    )
                live[("xt", n, a)] = xt

        def regroup(n):
            grp = work.tile([P, 2, 2, P, 4], BF16, name="grp", align_bytes=64)
            grp_words = grp[:].bitcast(F32)
            for a in range(2):
                nc.scalar.copy(
                    out=grp_words[:, a], in_=live[("xt", n, a)][:].rearrange("p (g u) r -> p g r u", u=2)
                )
            live[("grp", n)] = grp

        def quantise(n, pieces):
            grp = live[("grp", n)][:].rearrange("p a g r t -> p (a g r t)")
            codes = work.tile([P, 512], U32, name="codes", align_bytes=64)
            scales = work.tile([P, 512], U8, name="scales", align_bytes=64)
            width = 512 // pieces
            for piece in range(pieces):
                cols = slice(piece * width, (piece + 1) * width)
                nc.vector.quantize_mx(
                    out=codes[:, cols].bitcast(FP8X4),
                    scales=scales[:, cols],
                    in_=grp[:, 4 * piece * width : 4 * (piece + 1) * width],
                )
            live[("q", n)] = (codes, scales)

        def multiply(n):
            codes, scales = live[("q", n)]
            rope = ps_r.tile([P, 512], F32, name="rope")
            nope = ps_n.tile([P, 512], F32, name="nope")
            for s, bank in ((ROPE, rope), (NOPE, nope)):
                for a in range(2):
                    for g in range(2):
                        col = (2 * a + g) * P
                        nc.tensor.matmul_mx(
                            out=bank[:, 256 * a : 256 * a + 256],
                            lhsT=codes[:, col : col + P].bitcast(FP8X4),
                            lhsT_scale=scales[:, col : col + P],
                            rhs=wcodes[:, g, 256 * s : 256 * s + 256].bitcast(FP8X4),
                            rhs_scale=wscales[:, g, 256 * s : 256 * s + 256],
                            start=(g == 0),
                            stop=(g == 1),
                        )
            live[("rope", n)] = rope
            live[("nope", n)] = nope

        def plain_out(n):
            b, t0 = where(n)
            dst = out_of[n].rearrange("p q (a h s c) -> p q a h s c", a=2, h=2, s=2)
            nc.scalar.copy(
                out=dst[:, :, :, :, 0, :],
                in_=live[("nope", n)][:].rearrange("p (a q h c) -> p q a h c", a=2, q=2, h=2),
            )

        def products(n):
            b, t0 = where(n)
            rope = live[("rope", n)]
            dst = out_of[n].rearrange("p q (a h s c) -> p q a h s c", a=2, h=2, s=2)
            nc.vector.tensor_tensor(
                out=dst[:, :, :, :, 1, :],
                in0=rope[:].rearrange("p (a q h c) -> p q a h c", a=2, q=2, h=2),
                in1=cos_t[:, t0 : t0 + 2].unsqueeze(1).to_broadcast([P, 2, 2, 2, 2 * NPAIRS]),
                op=ALU.mult,
            )
            cross = work.tile([P, 2, 2, 2 * NPAIRS, 2], F32, name="cross")
            nc.vector.tensor_tensor(
                out=cross[:],
                in0=rope[:].rearrange("p (a q hi e) -> p a q hi e", a=2, q=2, e=2)[:, :, :, :, ::-1],
                in1=sin_t[:, t0 : t0 + 2]
                .rearrange("p a h i e -> p a (h i) e")
                .unsqueeze(2)
                .to_broadcast([P, 2, 2, 2 * NPAIRS, 2]),
                op=ALU.mult,
            )
            live[("cross", n)] = cross

        def add_and_store(n):
            b, t0 = where(n)
            eng = nc.gpsimd if n < GP_ADD_UNTIL else nc.vector
            rot = out_of[n].rearrange("p q (a h s c) -> p q a h s c", a=2, h=2, s=2)
            eng.tensor_tensor(
                out=rot[:, :, :, :, 1, :],
                in0=rot[:, :, :, :, 1, :],
                in1=live[("cross", n)][:].rearrange("p a q (h i) e -> p q a h (i e)", h=2),
                op=ALU.add,
            )
            if n in last_of:
                og, group = last_of[n]
                gb, gt0 = where(group[0])
                for qk in range(2):
                    nc.sync.dma_start(
                        out=out_views[qk][gb][:, gt0 : gt0 + 2 * len(group), :].rearrange("p (u a) d -> p u (a d)", a=2),
                        in_=og[:, :, qk, :],
                    )

        def prepare(n, pieces):
            transposes(n)
            regroup(n)
            quantise(n, pieces)

        def finish(n):
            multiply(n)
            products(n)
            plain_out(n)
            add_and_store(n)

        prepare(0, 2)
        prepare(1, 1)
        tables()
        finish(0)
        prepare(2, 1)
        for n in range(1, N_UNITS):
            if n + 2 < N_UNITS:
                prepare(n + 2, 1)
            finish(n)
